import numpy as np
import ml_dtypes


def mxq(x, axis, fmt="e4m3"):
    dtype, down = {"e4m3": (ml_dtypes.float8_e4m3fn, 7), "e5m2": (ml_dtypes.float8_e5m2, 14)}[fmt]
    v = np.moveaxis(np.asarray(x, np.float32).astype(ml_dtypes.bfloat16).astype(np.float64), axis, -1)
    blocks = v.reshape(v.shape[:-1] + (-1, 32))
    amax = np.abs(blocks).max(-1, keepdims=True)
    byte = np.maximum(np.where(amax > 0, np.frexp(amax)[1] - 1 + 127, 0) - down, 1)
    scale = np.exp2(byte - 127.0)
    codes = (blocks / scale).astype(np.float32).astype(dtype).astype(np.float64)
    return np.moveaxis((codes * scale).reshape(v.shape), -1, axis)


WIDE = False


def mx_kscale(k):
    if not WIDE:
        return np.ones(k)
    levels = np.array([10, -10, 5, -5, 0])
    a = np.random.permutation(np.resize(levels, k // 512 * 4)).reshape(k // 512, 4)
    idx = np.arange(k)
    return np.exp2(a[idx // 512, idx % 128 // 32])


BF16 = ml_dtypes.bfloat16


def bf(x):
    return np.asarray(x, np.float32).astype(BF16)


def f64(x):
    return np.asarray(x).astype(np.float64)


E2M1 = np.array([0.0, 0.5, 1.0, 1.5, 2.0, 3.0, 4.0, 6.0, -0.0, -0.5, -1.0, -1.5, -2.0, -3.0, -4.0, -6.0])


def pack_weight(w, fmt):
    k, n = w.shape
    w = f64(bf(w)).reshape(k // 32, 32, n)
    amax = np.abs(w).max(1)
    if fmt == "e4m3":
        byte = np.frexp(amax)[1] - 1 + 127 - 7
    else:
        mant, ex = np.frexp(amax / 6.0)
        byte = np.where(mant > 0.5, ex, ex - 1) + 127
    byte = np.clip(np.where(amax > 0, byte, 1), 1, 254)
    scaled = (w * np.exp2(127.0 - byte)[:, None, :]).reshape(k, n).astype(np.float32)
    by_word = np.ascontiguousarray(scaled.reshape(k // 512, 128, 4, n).transpose(0, 1, 3, 2))
    if fmt == "e4m3":
        words = by_word.astype(ml_dtypes.float8_e4m3fn).view(np.uint8)
    else:
        c = by_word.astype(ml_dtypes.float4_e2m1fn).view(np.uint8) & 0xF
        words = c[..., 0::2] | (c[..., 1::2] << 4)
    return np.ascontiguousarray(words), np.ascontiguousarray(byte.astype(np.uint8).reshape(k // 512, 16, n))


def unpack_weight(words, scales, fmt):
    g, p, n, _ = words.shape
    if fmt == "e4m3":
        vals = np.ascontiguousarray(words).view(ml_dtypes.float8_e4m3fn).astype(np.float64)
    else:
        nib = np.empty((g, p, n, 4), np.uint8)
        nib[..., 0::2] = words & 0xF
        nib[..., 1::2] = words >> 4
        vals = E2M1[nib]
    vals = vals * np.repeat(np.exp2(scales.astype(np.float64) - 127.0), 8, axis=1)[..., None]
    return vals.transpose(0, 1, 3, 2).reshape(g * 512, n)


B, C, H, W = 8, 512, 16, 16
HW = H * W
N = B * HW


def setup_inputs():
    s = mx_kscale(C)
    x = bf(np.random.standard_normal((B, C, H, W)) * s[None, :, None, None])
    w_g = np.random.standard_normal((C, C)) * 0.5 / np.sqrt(C) / s[None, :]
    words, scales = pack_weight(np.ascontiguousarray(w_g.T), "e4m3")
    return {"x": x, "w_g_words": words, "w_g_scales": scales}


def reference(x, w_g_words, w_g_scales):
    xf = f64(x).reshape(B, C, HW).transpose(0, 2, 1)
    g = mxq(xf, 2, "e4m3") @ unpack_weight(w_g_words, w_g_scales, "e4m3")
    gq = mxq(g, 2, "e4m3").reshape(N, C)
    p = (gq @ gq.T).reshape(B, HW, B, HW)
    gmax = p.max(axis=2)
    return gmax.transpose(1, 0, 2)

@@ -1,0 +1,152 @@
+from contextlib import ExitStack
+
+import concourse.mybir as mybir
+
+BF16 = mybir.dt.bfloat16
+F32 = mybir.dt.float32
+I32 = mybir.dt.int32
+U32 = mybir.dt.uint32
+U8 = mybir.dt.uint8
+FP8X4 = mybir.dt.float8_e4m3fn_x4
+MAX = mybir.AluOpType.max
+
+P = 128
+PACK = 4
+IMAGES = 8
+CHANNELS = P * PACK
+PIXELS = 256
+HALVES = PIXELS // P
+CHUNK_IMAGES = 2
+CHUNK = CHUNK_IMAGES * PIXELS
+CHUNKS = IMAGES // CHUNK_IMAGES
+AHEAD = 2
+RUN = 4
+
+FLOPS = 2 * IMAGES * PIXELS * CHANNELS * CHANNELS + 2 * (IMAGES * PIXELS) ** 2 * CHANNELS
+
+
+def tile_nlgp_pa_kernel(tc, x, w_g_words, w_g_scales, out):
+    nc = tc.nc
+    with ExitStack() as ctx:
+        ctx.enter_context(tc.manual_schedule())
+        keep = ctx.enter_context(tc.tile_pool(name="keep", bufs=1))
+        per_chunk = ctx.enter_context(tc.tile_pool(name="per_chunk", bufs=CHUNKS))
+        results = ctx.enter_context(tc.tile_pool(name="results", bufs=3))
+        psum_g = ctx.enter_context(tc.psum_pool(name="psum_g", bufs=2))
+        psum_p = ctx.enter_context(tc.psum_pool(name="psum_p", bufs=6))
+
+        w_words = keep.tile([P, CHANNELS], U32, align_bytes=64)
+        w_scales = keep.tile([P, CHANNELS], U8, align_bytes=64)
+        x_words = keep.tile([P, IMAGES * PIXELS], U32, align_bytes=64)
+        x_scales = keep.tile([P, IMAGES * PIXELS], U8, align_bytes=64)
+        g_words = keep.tile([P, IMAGES * PIXELS], U32, align_bytes=64)
+        g_scales = keep.tile([P, IMAGES * PIXELS], U8, align_bytes=64)
+        best = keep.tile([P, IMAGES * HALVES, CHUNK], F32)
+
+        nc.vector.memset(w_scales[:].bitcast(I32), 0)
+        x_by_word = x.rearrange("b (p t) h w -> p b (t h w)", t=PACK)
+        x_raw = []
+        for c in range(CHUNKS):
+            raw = per_chunk.tile([P, CHUNK_IMAGES, PACK * PIXELS], BF16, name="x_raw")
+            nc.sync.dma_start(out=raw[:], in_=x_by_word[:, c * CHUNK_IMAGES : (c + 1) * CHUNK_IMAGES, :])
+            x_raw.append(raw)
+            if c == 0:
+                for quadrant in range(4):
+                    nc.sync.dma_start(
+                        out=w_scales[32 * quadrant : 32 * quadrant + 4, :].bitcast(I32),
+                        in_=w_g_scales[0, 4 * quadrant : 4 * quadrant + 4, :].bitcast(I32),
+                    )
+                nc.sync.dma_start(
+                    out=w_words[:].bitcast(I32),
+                    in_=w_g_words[0].rearrange("p d t -> p (d t)").bitcast(I32),
+                )
+
+        def chunk_columns(c):
+            return slice(c * CHUNK, (c + 1) * CHUNK)
+
+        def quantise_x(c):
+            grouped = per_chunk.tile([P, CHUNK * PACK], BF16, name="x_grouped", align_bytes=64)
+            for b in range(CHUNK_IMAGES):
+                nc.vector.tensor_copy(
+                    out=grouped[:, b * PIXELS * PACK : (b + 1) * PIXELS * PACK].rearrange(
+                        "p (s i t) -> p s t i", i=RUN, t=PACK
+                    ),
+                    in_=x_raw[c][:, b, :].rearrange("p (t s i) -> p s t i", t=PACK, i=RUN),
+                )
+            nc.vector.quantize_mx(
+                out=x_words[:, chunk_columns(c)].bitcast(FP8X4),
+                scales=x_scales[:, chunk_columns(c)],
+                in_=grouped[:],
+            )
+
+        g_grouped = {}
+
+        def project(c):
+            g_grouped[c] = per_chunk.tile([P, CHUNK, PACK], BF16, name="g_grouped", align_bytes=64)
+            for s in range(CHUNK // P):
+                bank = psum_g.tile([P, PACK, P], F32)
+                pixels = slice(c * CHUNK + s * P, c * CHUNK + (s + 1) * P)
+                for t in range(PACK):
+                    d_tile = slice(t * P, (t + 1) * P)
+                    nc.tensor.matmul_mx(
+                        out=bank[:, t, :],
+                        lhsT=w_words[:, d_tile].bitcast(FP8X4),
+                        lhsT_scale=w_scales[:, d_tile],
+                        rhs=x_words[:, pixels].bitcast(FP8X4),
+                        rhs_scale=x_scales[:, pixels],
+                        start=True,
+                        stop=True,
+                    )
+                nc.scalar.copy(
+                    out=g_grouped[c][:, s * P : (s + 1) * P, :],
+                    in_=bank[:].rearrange("p t n -> p n t"),
+                )
+
+        def quantise_g(c):
+            nc.vector.quantize_mx(
+                out=g_words[:, chunk_columns(c)].bitcast(FP8X4),
+                scales=g_scales[:, chunk_columns(c)],
+                in_=g_grouped[c][:].rearrange("p n t -> p (n t)"),
+            )
+
+        def fold(r, c):
+            rows = slice(r * P, (r + 1) * P)
+            bank = psum_p.tile([P, CHUNK], F32)
+            nc.tensor.matmul_mx(
+                out=bank[:],
+                lhsT=g_words[:, rows].bitcast(FP8X4),
+                lhsT_scale=g_scales[:, rows],
+                rhs=g_words[:, chunk_columns(c)].bitcast(FP8X4),
+                rhs_scale=g_scales[:, chunk_columns(c)],
+                start=True,
+                stop=True,
+            )
+            if c == 0:
+                nc.scalar.copy(out=best[:, r, :], in_=bank[:])
+            else:
+                nc.vector.tensor_tensor(out=best[:, r, :], in0=bank[:], in1=best[:, r, :], op=MAX)
+
+        def finish(b):
+            rows = slice(b * HALVES, (b + 1) * HALVES)
+            result = results.tile([P, HALVES, PIXELS], F32)
+            nc.vector.tensor_tensor(
+                out=result[:], in0=best[:, rows, 0:PIXELS], in1=best[:, rows, PIXELS:CHUNK], op=MAX
+            )
+            nc.sync.dma_start(out=out[:, b, :].rearrange("(h p) j -> p h j", p=P), in_=result[:])
+
+        for c in range(CHUNKS):
+            quantise_x(c)
+        for c in range(AHEAD):
+            project(c)
+        for c in range(CHUNKS):
+            quantise_g(c)
+            for b in range((c + 1) * CHUNK_IMAGES):
+                partners = [c] if b < c * CHUNK_IMAGES else range(c + 1)
+                for partner in partners:
+                    for h in range(HALVES):
+                        fold(b * HALVES + h, partner)
+                if c == CHUNKS - 1 and b > 0:
+                    finish(b - 1)
+            if c + AHEAD < CHUNKS:
+                project(c + AHEAD)
+        finish(IMAGES - 1)

@@ -19,7 +19,6 @@ HALVES = PIXELS // P
 CHUNK_IMAGES = 2
 CHUNK = CHUNK_IMAGES * PIXELS
 CHUNKS = IMAGES // CHUNK_IMAGES
-AHEAD = 2
 RUN = 4
 
 FLOPS = 2 * IMAGES * PIXELS * CHANNELS * CHANNELS + 2 * (IMAGES * PIXELS) ** 2 * CHANNELS
@@ -31,6 +30,7 @@ def tile_nlgp_pa_kernel(tc, x, w_g_words, w_g_scales, out):
         ctx.enter_context(tc.manual_schedule())
         keep = ctx.enter_context(tc.tile_pool(name="keep", bufs=1))
         per_chunk = ctx.enter_context(tc.tile_pool(name="per_chunk", bufs=CHUNKS))
+        per_image = ctx.enter_context(tc.tile_pool(name="per_image", bufs=IMAGES))
         results = ctx.enter_context(tc.tile_pool(name="results", bufs=3))
         psum_g = ctx.enter_context(tc.psum_pool(name="psum_g", bufs=2))
         psum_p = ctx.enter_context(tc.psum_pool(name="psum_p", bufs=6))
@@ -46,11 +46,11 @@ def tile_nlgp_pa_kernel(tc, x, w_g_words, w_g_scales, out):
         nc.vector.memset(w_scales[:].bitcast(I32), 0)
         x_by_word = x.rearrange("b (p t) h w -> p b (t h w)", t=PACK)
         x_raw = []
-        for c in range(CHUNKS):
-            raw = per_chunk.tile([P, CHUNK_IMAGES, PACK * PIXELS], BF16, name="x_raw")
-            nc.sync.dma_start(out=raw[:], in_=x_by_word[:, c * CHUNK_IMAGES : (c + 1) * CHUNK_IMAGES, :])
+        for b in range(IMAGES):
+            raw = per_image.tile([P, PACK * PIXELS], BF16, name="x_raw")
+            nc.sync.dma_start(out=raw[:], in_=x_by_word[:, b, :])
             x_raw.append(raw)
-            if c == 0:
+            if b == CHUNK_IMAGES - 1:
                 for quadrant in range(4):
                     nc.sync.dma_start(
                         out=w_scales[32 * quadrant : 32 * quadrant + 4, :].bitcast(I32),
@@ -71,7 +71,7 @@ def tile_nlgp_pa_kernel(tc, x, w_g_words, w_g_scales, out):
                     out=grouped[:, b * PIXELS * PACK : (b + 1) * PIXELS * PACK].rearrange(
                         "p (s i t) -> p s t i", i=RUN, t=PACK
                     ),
-                    in_=x_raw[c][:, b, :].rearrange("p (t s i) -> p s t i", t=PACK, i=RUN),
+                    in_=x_raw[c * CHUNK_IMAGES + b][:].rearrange("p (t s i) -> p s t i", t=PACK, i=RUN),
                 )
             nc.vector.quantize_mx(
                 out=x_words[:, chunk_columns(c)].bitcast(FP8X4),
@@ -134,19 +134,28 @@ def tile_nlgp_pa_kernel(tc, x, w_g_words, w_g_scales, out):
             )
             nc.sync.dma_start(out=out[:, b, :].rearrange("(h p) j -> p h j", p=P), in_=result[:])
 
+        def meet(b, partners):
+            for partner in partners:
+                for h in range(HALVES):
+                    fold(b * HALVES + h, partner)
+
+        quantise_x(0)
+        project(0)
+        quantise_x(1)
+        quantise_g(0)
         for c in range(CHUNKS):
-            quantise_x(c)
-        for c in range(AHEAD):
-            project(c)
-        for c in range(CHUNKS):
-            quantise_g(c)
-            for b in range((c + 1) * CHUNK_IMAGES):
-                partners = [c] if b < c * CHUNK_IMAGES else range(c + 1)
-                for partner in partners:
-                    for h in range(HALVES):
-                        fold(b * HALVES + h, partner)
-                if c == CHUNKS - 1 and b > 0:
+            last = c == CHUNKS - 1
+            for b in range(c * CHUNK_IMAGES):
+                meet(b, [c])
+                if last and b > 0:
                     finish(b - 1)
-            if c + AHEAD < CHUNKS:
-                project(c + AHEAD)
+            if c + 2 < CHUNKS:
+                quantise_x(c + 2)
+            if c + 1 < CHUNKS:
+                project(c + 1)
+                quantise_g(c + 1)
+            for b in range(c * CHUNK_IMAGES, (c + 1) * CHUNK_IMAGES):
+                meet(b, range(c + 1))
+                if last:
+                    finish(b - 1)
         finish(IMAGES - 1)

@@ -29,7 +29,6 @@ def tile_nlgp_pa_kernel(tc, x, w_g_words, w_g_scales, out):
     with ExitStack() as ctx:
         ctx.enter_context(tc.manual_schedule())
         keep = ctx.enter_context(tc.tile_pool(name="keep", bufs=1))
-        per_chunk = ctx.enter_context(tc.tile_pool(name="per_chunk", bufs=CHUNKS))
         per_image = ctx.enter_context(tc.tile_pool(name="per_image", bufs=IMAGES))
         results = ctx.enter_context(tc.tile_pool(name="results", bufs=3))
         psum_g = ctx.enter_context(tc.psum_pool(name="psum_g", bufs=2))
@@ -50,7 +49,7 @@ def tile_nlgp_pa_kernel(tc, x, w_g_words, w_g_scales, out):
             raw = per_image.tile([P, PACK * PIXELS], BF16, name="x_raw")
             nc.sync.dma_start(out=raw[:], in_=x_by_word[:, b, :])
             x_raw.append(raw)
-            if b == CHUNK_IMAGES - 1:
+            if b == 0:
                 for quadrant in range(4):
                     nc.sync.dma_start(
                         out=w_scales[32 * quadrant : 32 * quadrant + 4, :].bitcast(I32),
@@ -61,31 +60,37 @@ def tile_nlgp_pa_kernel(tc, x, w_g_words, w_g_scales, out):
                     in_=w_g_words[0].rearrange("p d t -> p (d t)").bitcast(I32),
                 )
 
+        def image_columns(b):
+            return slice(b * PIXELS, (b + 1) * PIXELS)
+
         def chunk_columns(c):
             return slice(c * CHUNK, (c + 1) * CHUNK)
 
-        def quantise_x(c):
-            grouped = per_chunk.tile([P, CHUNK * PACK], BF16, name="x_grouped", align_bytes=64)
-            for b in range(CHUNK_IMAGES):
-                nc.vector.tensor_copy(
-                    out=grouped[:, b * PIXELS * PACK : (b + 1) * PIXELS * PACK].rearrange(
-                        "p (s i t) -> p s t i", i=RUN, t=PACK
-                    ),
-                    in_=x_raw[c * CHUNK_IMAGES + b][:].rearrange("p (t s i) -> p s t i", t=PACK, i=RUN),
-                )
-            nc.vector.quantize_mx(
-                out=x_words[:, chunk_columns(c)].bitcast(FP8X4),
-                scales=x_scales[:, chunk_columns(c)],
-                in_=grouped[:],
-            )
+        def chunk_images(c):
+            return range(c * CHUNK_IMAGES, (c + 1) * CHUNK_IMAGES)
 
+        x_grouped = {}
         g_grouped = {}
 
-        def project(c):
-            g_grouped[c] = per_chunk.tile([P, CHUNK, PACK], BF16, name="g_grouped", align_bytes=64)
-            for s in range(CHUNK // P):
+        def regroup_x(b):
+            x_grouped[b] = per_image.tile([P, PIXELS * PACK], BF16, name="x_grouped", align_bytes=64)
+            nc.vector.tensor_copy(
+                out=x_grouped[b][:].rearrange("p (s i t) -> p s t i", i=RUN, t=PACK),
+                in_=x_raw[b][:].rearrange("p (t s i) -> p s t i", t=PACK, i=RUN),
+            )
+
+        def quantise_x(b):
+            nc.vector.quantize_mx(
+                out=x_words[:, image_columns(b)].bitcast(FP8X4),
+                scales=x_scales[:, image_columns(b)],
+                in_=x_grouped[b][:],
+            )
+
+        def project(b):
+            g_grouped[b] = per_image.tile([P, PIXELS, PACK], BF16, name="g_grouped", align_bytes=64)
+            for h in range(HALVES):
                 bank = psum_g.tile([P, PACK, P], F32)
-                pixels = slice(c * CHUNK + s * P, c * CHUNK + (s + 1) * P)
+                pixels = slice(b * PIXELS + h * P, b * PIXELS + (h + 1) * P)
                 for t in range(PACK):
                     d_tile = slice(t * P, (t + 1) * P)
                     nc.tensor.matmul_mx(
@@ -98,16 +103,26 @@ def tile_nlgp_pa_kernel(tc, x, w_g_words, w_g_scales, out):
                         stop=True,
                     )
                 nc.scalar.copy(
-                    out=g_grouped[c][:, s * P : (s + 1) * P, :],
-                    in_=bank[:].rearrange("p t n -> p n t"),
+                    out=g_grouped[b][:, h * P : (h + 1) * P, :],
+                    in_=bank[:].rearrange("p t i -> p i t"),
                 )
 
-        def quantise_g(c):
+        def quantise_g(b):
             nc.vector.quantize_mx(
-                out=g_words[:, chunk_columns(c)].bitcast(FP8X4),
-                scales=g_scales[:, chunk_columns(c)],
-                in_=g_grouped[c][:].rearrange("p n t -> p (n t)"),
+                out=g_words[:, image_columns(b)].bitcast(FP8X4),
+                scales=g_scales[:, image_columns(b)],
+                in_=g_grouped[b][:].rearrange("p i t -> p (i t)"),
             )
+
+        def prepare(c):
+            for b in chunk_images(c):
+                project(b)
+            for b in chunk_images(c):
+                if c + 1 < CHUNKS:
+                    regroup_x(b + CHUNK_IMAGES)
+                quantise_g(b)
+                if c + 1 < CHUNKS:
+                    quantise_x(b + CHUNK_IMAGES)
 
         def fold(r, c):
             rows = slice(r * P, (r + 1) * P)
@@ -126,6 +141,11 @@ def tile_nlgp_pa_kernel(tc, x, w_g_words, w_g_scales, out):
             else:
                 nc.vector.tensor_tensor(out=best[:, r, :], in0=bank[:], in1=best[:, r, :], op=MAX)
 
+        def meet(b, partners):
+            for partner in partners:
+                for h in range(HALVES):
+                    fold(b * HALVES + h, partner)
+
         def finish(b):
             rows = slice(b * HALVES, (b + 1) * HALVES)
             result = results.tile([P, HALVES, PIXELS], F32)
@@ -134,27 +154,19 @@ def tile_nlgp_pa_kernel(tc, x, w_g_words, w_g_scales, out):
             )
             nc.sync.dma_start(out=out[:, b, :].rearrange("(h p) j -> p h j", p=P), in_=result[:])
 
-        def meet(b, partners):
-            for partner in partners:
-                for h in range(HALVES):
-                    fold(b * HALVES + h, partner)
-
-        quantise_x(0)
-        project(0)
-        quantise_x(1)
-        quantise_g(0)
+        for b in chunk_images(0):
+            regroup_x(b)
+            quantise_x(b)
+        prepare(0)
         for c in range(CHUNKS):
             last = c == CHUNKS - 1
             for b in range(c * CHUNK_IMAGES):
                 meet(b, [c])
                 if last and b > 0:
                     finish(b - 1)
-            if c + 2 < CHUNKS:
-                quantise_x(c + 2)
-            if c + 1 < CHUNKS:
-                project(c + 1)
-                quantise_g(c + 1)
-            for b in range(c * CHUNK_IMAGES, (c + 1) * CHUNK_IMAGES):
+            if not last:
+                prepare(c + 1)
+            for b in chunk_images(c):
                 meet(b, range(c + 1))
                 if last:
                     finish(b - 1)

@@ -19,6 +19,8 @@ HALVES = PIXELS // P
 CHUNK_IMAGES = 2
 CHUNK = CHUNK_IMAGES * PIXELS
 CHUNKS = IMAGES // CHUNK_IMAGES
+EARLY_IMAGES = 4
+X_AHEAD = 3
 RUN = 4
 
 FLOPS = 2 * IMAGES * PIXELS * CHANNELS * CHANNELS + 2 * (IMAGES * PIXELS) ** 2 * CHANNELS
@@ -31,8 +33,7 @@ def tile_nlgp_pa_kernel(tc, x, w_g_words, w_g_scales, out):
         keep = ctx.enter_context(tc.tile_pool(name="keep", bufs=1))
         per_image = ctx.enter_context(tc.tile_pool(name="per_image", bufs=IMAGES))
         results = ctx.enter_context(tc.tile_pool(name="results", bufs=3))
-        psum_g = ctx.enter_context(tc.psum_pool(name="psum_g", bufs=2))
-        psum_p = ctx.enter_context(tc.psum_pool(name="psum_p", bufs=6))
+        psum = ctx.enter_context(tc.psum_pool(name="psum", bufs=8))
 
         w_words = keep.tile([P, CHANNELS], U32, align_bytes=64)
         w_scales = keep.tile([P, CHANNELS], U8, align_bytes=64)
@@ -89,7 +90,7 @@ def tile_nlgp_pa_kernel(tc, x, w_g_words, w_g_scales, out):
         def project(b):
             g_grouped[b] = per_image.tile([P, PIXELS, PACK], BF16, name="g_grouped", align_bytes=64)
             for h in range(HALVES):
-                bank = psum_g.tile([P, PACK, P], F32)
+                bank = psum.tile([P, PACK, P], F32, tag="bank")
                 pixels = slice(b * PIXELS + h * P, b * PIXELS + (h + 1) * P)
                 for t in range(PACK):
                     d_tile = slice(t * P, (t + 1) * P)
@@ -114,19 +115,9 @@ def tile_nlgp_pa_kernel(tc, x, w_g_words, w_g_scales, out):
                 in_=g_grouped[b][:].rearrange("p i t -> p (i t)"),
             )
 
-        def prepare(c):
-            for b in chunk_images(c):
-                project(b)
-            for b in chunk_images(c):
-                if c + 1 < CHUNKS:
-                    regroup_x(b + CHUNK_IMAGES)
-                quantise_g(b)
-                if c + 1 < CHUNKS:
-                    quantise_x(b + CHUNK_IMAGES)
-
         def fold(r, c):
             rows = slice(r * P, (r + 1) * P)
-            bank = psum_p.tile([P, CHUNK], F32)
+            bank = psum.tile([P, CHUNK], F32, tag="bank")
             nc.tensor.matmul_mx(
                 out=bank[:],
                 lhsT=g_words[:, rows].bitcast(FP8X4),
@@ -154,20 +145,25 @@ def tile_nlgp_pa_kernel(tc, x, w_g_words, w_g_scales, out):
             )
             nc.sync.dma_start(out=out[:, b, :].rearrange("(h p) j -> p h j", p=P), in_=result[:])
 
-        for b in chunk_images(0):
+        for b in range(X_AHEAD):
             regroup_x(b)
             quantise_x(b)
-        prepare(0)
-        for c in range(CHUNKS):
-            last = c == CHUNKS - 1
-            for b in range(c * CHUNK_IMAGES):
-                meet(b, [c])
-                if last and b > 0:
-                    finish(b - 1)
-            if not last:
-                prepare(c + 1)
-            for b in chunk_images(c):
-                meet(b, range(c + 1))
-                if last:
-                    finish(b - 1)
-        finish(IMAGES - 1)
+        for b in range((CHUNKS - 1) * CHUNK_IMAGES):
+            project(b)
+            if b + X_AHEAD < IMAGES:
+                regroup_x(b + X_AHEAD)
+            quantise_g(b)
+            if b + X_AHEAD < IMAGES:
+                quantise_x(b + X_AHEAD)
+        for b in range(EARLY_IMAGES):
+            meet(b, range(CHUNKS - 1))
+        for b in chunk_images(CHUNKS - 1):
+            project(b)
+        for b in chunk_images(CHUNKS - 1):
+            quantise_g(b)
+        closing = list(range(EARLY_IMAGES, IMAGES)) + list(range(EARLY_IMAGES))
+        for k, b in enumerate(closing):
+            meet(b, range(CHUNKS) if b >= EARLY_IMAGES else [CHUNKS - 1])
+            if k > 0:
+                finish(closing[k - 1])
+        finish(closing[-1])

@@ -9,6 +9,9 @@ U32 = mybir.dt.uint32
 U8 = mybir.dt.uint8
 FP8X4 = mybir.dt.float8_e4m3fn_x4
 MAX = mybir.AluOpType.max
+MULT = mybir.AluOpType.mult
+ADD = mybir.AluOpType.add
+RELU = mybir.ActivationFunctionType.Relu
 
 P = 128
 PACK = 4
@@ -16,10 +19,9 @@ IMAGES = 8
 CHANNELS = P * PACK
 PIXELS = 256
 HALVES = PIXELS // P
-CHUNK_IMAGES = 2
-CHUNK = CHUNK_IMAGES * PIXELS
-CHUNKS = IMAGES // CHUNK_IMAGES
-EARLY_IMAGES = 4
+BANK = HALVES * PIXELS
+PAIRS = ((0, 1), (2, 3), (4, 5))
+PAIRS_OF = (1, 1, 3, 3, 3, 2, 2, 2)
 X_AHEAD = 3
 RUN = 4
 
@@ -29,11 +31,13 @@ FLOPS = 2 * IMAGES * PIXELS * CHANNELS * CHANNELS + 2 * (IMAGES * PIXELS) ** 2 *
 def tile_nlgp_pa_kernel(tc, x, w_g_words, w_g_scales, out):
     nc = tc.nc
     with ExitStack() as ctx:
-        ctx.enter_context(tc.manual_schedule())
         keep = ctx.enter_context(tc.tile_pool(name="keep", bufs=1))
         per_image = ctx.enter_context(tc.tile_pool(name="per_image", bufs=IMAGES))
+        work = ctx.enter_context(tc.tile_pool(name="work", bufs=4))
+        bests = ctx.enter_context(tc.tile_pool(name="bests", bufs=12))
         results = ctx.enter_context(tc.tile_pool(name="results", bufs=3))
-        psum = ctx.enter_context(tc.psum_pool(name="psum", bufs=8))
+        scalar_banks = ctx.enter_context(tc.psum_pool(name="scalar_banks", bufs=4))
+        vector_banks = ctx.enter_context(tc.psum_pool(name="vector_banks", bufs=4))
 
         w_words = keep.tile([P, CHANNELS], U32, align_bytes=64)
         w_scales = keep.tile([P, CHANNELS], U8, align_bytes=64)
@@ -41,9 +45,16 @@ def tile_nlgp_pa_kernel(tc, x, w_g_words, w_g_scales, out):
         x_scales = keep.tile([P, IMAGES * PIXELS], U8, align_bytes=64)
         g_words = keep.tile([P, IMAGES * PIXELS], U32, align_bytes=64)
         g_scales = keep.tile([P, IMAGES * PIXELS], U8, align_bytes=64)
-        best = keep.tile([P, IMAGES * HALVES, CHUNK], F32)
+        neg_words = {}
+        neg_scales = {}
+        for pair in PAIRS:
+            neg_words[pair[1]] = keep.tile([P, PIXELS], U32, name="neg_words%d" % pair[1], align_bytes=64)
+            neg_scales[pair[1]] = keep.tile([P, PIXELS], U8, name="neg_scales%d" % pair[1], align_bytes=64)
+        warm = keep.tile([P, 8], F32)
 
         nc.vector.memset(w_scales[:].bitcast(I32), 0)
+        nc.vector.memset(warm[:], 0.0)
+        nc.scalar.activation(out=warm[:], in_=warm[:], func=RELU)
         x_by_word = x.rearrange("b (p t) h w -> p b (t h w)", t=PACK)
         x_raw = []
         for b in range(IMAGES):
@@ -64,14 +75,9 @@ def tile_nlgp_pa_kernel(tc, x, w_g_words, w_g_scales, out):
         def image_columns(b):
             return slice(b * PIXELS, (b + 1) * PIXELS)
 
-        def chunk_columns(c):
-            return slice(c * CHUNK, (c + 1) * CHUNK)
-
-        def chunk_images(c):
-            return range(c * CHUNK_IMAGES, (c + 1) * CHUNK_IMAGES)
-
         x_grouped = {}
         g_grouped = {}
+        g_negated = {}
 
         def regroup_x(b):
             x_grouped[b] = per_image.tile([P, PIXELS * PACK], BF16, name="x_grouped", align_bytes=64)
@@ -90,7 +96,7 @@ def tile_nlgp_pa_kernel(tc, x, w_g_words, w_g_scales, out):
         def project(b):
             g_grouped[b] = per_image.tile([P, PIXELS, PACK], BF16, name="g_grouped", align_bytes=64)
             for h in range(HALVES):
-                bank = psum.tile([P, PACK, P], F32, tag="bank")
+                bank = scalar_banks.tile([P, PACK, P], F32, tag="bank")
                 pixels = slice(b * PIXELS + h * P, b * PIXELS + (h + 1) * P)
                 for t in range(PACK):
                     d_tile = slice(t * P, (t + 1) * P)
@@ -115,55 +121,140 @@ def tile_nlgp_pa_kernel(tc, x, w_g_words, w_g_scales, out):
                 in_=g_grouped[b][:].rearrange("p i t -> p (i t)"),
             )
 
-        def fold(r, c):
-            rows = slice(r * P, (r + 1) * P)
-            bank = psum.tile([P, CHUNK], F32, tag="bank")
-            nc.tensor.matmul_mx(
-                out=bank[:],
-                lhsT=g_words[:, rows].bitcast(FP8X4),
-                lhsT_scale=g_scales[:, rows],
-                rhs=g_words[:, chunk_columns(c)].bitcast(FP8X4),
-                rhs_scale=g_scales[:, chunk_columns(c)],
-                start=True,
-                stop=True,
+        def negate_g(b):
+            g_negated[b] = keep.tile([P, PIXELS * PACK], BF16, name="g_negated%d" % b, align_bytes=64)
+            nc.vector.tensor_scalar(
+                out=g_negated[b][:], in0=g_grouped[b][:].rearrange("p i t -> p (i t)"), scalar1=-1.0, scalar2=None, op0=MULT
             )
-            if c == 0:
-                nc.scalar.copy(out=best[:, r, :], in_=bank[:])
-            else:
-                nc.vector.tensor_tensor(out=best[:, r, :], in0=bank[:], in1=best[:, r, :], op=MAX)
 
-        def meet(b, partners):
-            for partner in partners:
-                for h in range(HALVES):
-                    fold(b * HALVES + h, partner)
+        def quantise_negated(b):
+            nc.vector.quantize_mx(
+                out=neg_words[b][:].bitcast(FP8X4),
+                scales=neg_scales[b][:],
+                in_=g_negated[b][:],
+            )
+
+        def multiply(bank, b, partner, minus=None):
+            for h in range(HALVES):
+                rows = slice(b * PIXELS + h * P, b * PIXELS + (h + 1) * P)
+                nc.tensor.matmul_mx(
+                    out=bank[:, h, :],
+                    lhsT=g_words[:, rows].bitcast(FP8X4),
+                    lhsT_scale=g_scales[:, rows],
+                    rhs=g_words[:, image_columns(partner)].bitcast(FP8X4),
+                    rhs_scale=g_scales[:, image_columns(partner)],
+                    start=True,
+                    stop=minus is None,
+                )
+                if minus is not None:
+                    nc.tensor.matmul_mx(
+                        out=bank[:, h, :],
+                        lhsT=g_words[:, rows].bitcast(FP8X4),
+                        lhsT_scale=g_scales[:, rows],
+                        rhs=neg_words[minus][:].bitcast(FP8X4),
+                        rhs_scale=neg_scales[minus][:],
+                        start=False,
+                        stop=True,
+                    )
+
+        excess = {}
+        base = {}
+        best = {}
+
+        def pair_difference(b, q):
+            bank = scalar_banks.tile([P, HALVES, PIXELS], F32, tag="bank")
+            multiply(bank, b, PAIRS[q][0], minus=PAIRS[q][1])
+            excess[b, q] = work.tile([P, HALVES, PIXELS], F32, name="excess")
+            nc.scalar.activation(out=excess[b, q][:], in_=bank[:], func=RELU)
+
+        def pair_base(b, q):
+            bank = scalar_banks.tile([P, HALVES, PIXELS], F32, tag="bank")
+            multiply(bank, b, PAIRS[q][1])
+            base[b, q] = work.tile([P, HALVES, PIXELS], F32, name="base")
+            nc.scalar.copy(out=base[b, q][:], in_=bank[:])
+            best[b, q] = bests.tile([P, HALVES, PIXELS], F32, name="best")
+            nc.gpsimd.tensor_tensor(out=best[b, q][:], in0=excess[b, q][:], in1=base[b, q][:], op=ADD)
+
+        def fold(b, s):
+            bank = vector_banks.tile([P, HALVES, PIXELS], F32, tag="bank")
+            multiply(bank, b, s)
+            running = best[b, s % min(PAIRS_OF[b], 2)]
+            nc.vector.tensor_tensor(out=running[:], in0=bank[:], in1=running[:], op=MAX)
+
+        def join(b, q):
+            nc.vector.tensor_tensor(out=best[b, 0][:], in0=best[b, 0][:], in1=best[b, q][:], op=MAX)
+
+        def store(b):
+            nc.sync.dma_start(out=out[:, b, :].rearrange("(h p) j -> p h j", p=P), in_=best[b, 0][:])
 
         def finish(b):
-            rows = slice(b * HALVES, (b + 1) * HALVES)
-            result = results.tile([P, HALVES, PIXELS], F32)
-            nc.vector.tensor_tensor(
-                out=result[:], in0=best[:, rows, 0:PIXELS], in1=best[:, rows, PIXELS:CHUNK], op=MAX
-            )
-            nc.sync.dma_start(out=out[:, b, :].rearrange("(h p) j -> p h j", p=P), in_=result[:])
+            if PAIRS_OF[b] > 1:
+                join(b, 1)
+            store(b)
+
+        def pair_steps(b):
+            steps = []
+            for q in range(PAIRS_OF[b]):
+                steps.append((pair_difference, b, q))
+                steps.append((pair_base, b, q))
+            return steps
+
+        def run(steps, count):
+            for k in range(min(count, len(steps))):
+                step, b, q = steps[0]
+                steps.remove(steps[0])
+                step(b, q)
 
         for b in range(X_AHEAD):
             regroup_x(b)
             quantise_x(b)
-        for b in range((CHUNKS - 1) * CHUNK_IMAGES):
+        for b in range(4):
             project(b)
-            if b + X_AHEAD < IMAGES:
-                regroup_x(b + X_AHEAD)
+            regroup_x(b + X_AHEAD)
             quantise_g(b)
-            if b + X_AHEAD < IMAGES:
-                quantise_x(b + X_AHEAD)
-        for b in range(EARLY_IMAGES):
-            meet(b, range(CHUNKS - 1))
-        for b in chunk_images(CHUNKS - 1):
-            project(b)
-        for b in chunk_images(CHUNKS - 1):
-            quantise_g(b)
-        closing = list(range(EARLY_IMAGES, IMAGES)) + list(range(EARLY_IMAGES))
-        for k, b in enumerate(closing):
-            meet(b, range(CHUNKS) if b >= EARLY_IMAGES else [CHUNKS - 1])
-            if k > 0:
-                finish(closing[k - 1])
-        finish(closing[-1])
+            if b in neg_words:
+                negate_g(b)
+            quantise_x(b + X_AHEAD)
+            if b in neg_words:
+                quantise_negated(b)
+        run(pair_steps(0), 2)
+        regroup_x(7)
+        project(4)
+        fold(0, 2)
+        run(pair_steps(1), 2)
+        quantise_x(7)
+        quantise_g(4)
+        project(5)
+        fold(0, 3)
+        fold(1, 2)
+        quantise_g(5)
+        project(6)
+        fold(1, 3)
+        negate_g(5)
+        fold(0, 4)
+        quantise_negated(5)
+        fold(1, 4)
+        quantise_g(6)
+        project(7)
+        fold(0, 5)
+        fold(1, 5)
+        quantise_g(7)
+        ahead = []
+        for b in range(2, IMAGES):
+            ahead = ahead + pair_steps(b)
+        for s in (6, 7):
+            for b in (0, 1):
+                run(ahead, 1)
+                fold(b, s)
+        store(0)
+        store(1)
+        for b in range(2, IMAGES):
+            singles = list(range(2 * PAIRS_OF[b], IMAGES))
+            for k in range(len(singles)):
+                run(ahead, 1 if PAIRS_OF[b] == 2 else 3)
+                fold(b, singles[k])
+                if k == 0 and b > 2:
+                    finish(b - 1)
+            if PAIRS_OF[b] == 3:
+                join(b, 2)
+        finish(IMAGES - 1)

@@ -20,8 +20,8 @@ CHANNELS = P * PACK
 PIXELS = 256
 HALVES = PIXELS // P
 BANK = HALVES * PIXELS
-PAIRS = ((0, 1), (2, 3), (4, 5))
-PAIRS_OF = (1, 1, 3, 3, 3, 2, 2, 2)
+PAIRS = ((0, 1),)
+PAIRS_OF = (1,) * IMAGES
 X_AHEAD = 3
 RUN = 4
 
@@ -230,9 +230,7 @@ def tile_nlgp_pa_kernel(tc, x, w_g_words, w_g_scales, out):
         quantise_g(5)
         project(6)
         fold(1, 3)
-        negate_g(5)
         fold(0, 4)
-        quantise_negated(5)
         fold(1, 4)
         quantise_g(6)
         project(7)
@@ -248,13 +246,10 @@ def tile_nlgp_pa_kernel(tc, x, w_g_words, w_g_scales, out):
                 fold(b, s)
         store(0)
         store(1)
-        for b in range(2, IMAGES):
-            singles = list(range(2 * PAIRS_OF[b], IMAGES))
-            for k in range(len(singles)):
-                run(ahead, 1 if PAIRS_OF[b] == 2 else 3)
-                fold(b, singles[k])
-                if k == 0 and b > 2:
-                    finish(b - 1)
-            if PAIRS_OF[b] == 3:
-                join(b, 2)
-        finish(IMAGES - 1)
+        for b0 in range(2, IMAGES, 2):
+            for s in range(2, IMAGES):
+                for b in (b0, b0 + 1):
+                    run(ahead, 1)
+                    fold(b, s)
+            store(b0)
+            store(b0 + 1)

@@ -20,8 +20,7 @@ CHANNELS = P * PACK
 PIXELS = 256
 HALVES = PIXELS // P
 BANK = HALVES * PIXELS
-PAIRS = ((0, 1),)
-PAIRS_OF = (1,) * IMAGES
+PAIRS = ((0, 1), (2, 3))
 X_AHEAD = 3
 RUN = 4
 
@@ -31,11 +30,12 @@ FLOPS = 2 * IMAGES * PIXELS * CHANNELS * CHANNELS + 2 * (IMAGES * PIXELS) ** 2 *
 def tile_nlgp_pa_kernel(tc, x, w_g_words, w_g_scales, out):
     nc = tc.nc
     with ExitStack() as ctx:
+        pinned = {mybir.EngineType.DVE, mybir.EngineType.Activation, mybir.EngineType.Pool}
+        ctx.enter_context(tc.manual_schedule(engines=pinned))
         keep = ctx.enter_context(tc.tile_pool(name="keep", bufs=1))
         per_image = ctx.enter_context(tc.tile_pool(name="per_image", bufs=IMAGES))
         work = ctx.enter_context(tc.tile_pool(name="work", bufs=4))
-        bests = ctx.enter_context(tc.tile_pool(name="bests", bufs=12))
-        results = ctx.enter_context(tc.tile_pool(name="results", bufs=3))
+        bests = ctx.enter_context(tc.tile_pool(name="bests", bufs=16))
         scalar_banks = ctx.enter_context(tc.psum_pool(name="scalar_banks", bufs=4))
         vector_banks = ctx.enter_context(tc.psum_pool(name="vector_banks", bufs=4))
 
@@ -158,8 +158,13 @@ def tile_nlgp_pa_kernel(tc, x, w_g_words, w_g_scales, out):
                     )
 
         excess = {}
-        base = {}
         best = {}
+
+        def chain_start(b):
+            bank = scalar_banks.tile([P, HALVES, PIXELS], F32, tag="bank")
+            multiply(bank, b, 0)
+            best[b, 0] = bests.tile([P, HALVES, PIXELS], F32, name="best")
+            nc.scalar.copy(out=best[b, 0][:], in_=bank[:])
 
         def pair_difference(b, q):
             bank = scalar_banks.tile([P, HALVES, PIXELS], F32, tag="bank")
@@ -170,46 +175,33 @@ def tile_nlgp_pa_kernel(tc, x, w_g_words, w_g_scales, out):
         def pair_base(b, q):
             bank = scalar_banks.tile([P, HALVES, PIXELS], F32, tag="bank")
             multiply(bank, b, PAIRS[q][1])
-            base[b, q] = work.tile([P, HALVES, PIXELS], F32, name="base")
-            nc.scalar.copy(out=base[b, q][:], in_=bank[:])
+            base = work.tile([P, HALVES, PIXELS], F32, name="base")
+            nc.scalar.copy(out=base[:], in_=bank[:])
             best[b, q] = bests.tile([P, HALVES, PIXELS], F32, name="best")
-            nc.gpsimd.tensor_tensor(out=best[b, q][:], in0=excess[b, q][:], in1=base[b, q][:], op=ADD)
+            nc.gpsimd.tensor_tensor(out=best[b, q][:], in0=excess[b, q][:], in1=base[:], op=ADD)
 
         def fold(b, s):
             bank = vector_banks.tile([P, HALVES, PIXELS], F32, tag="bank")
             multiply(bank, b, s)
-            running = best[b, s % min(PAIRS_OF[b], 2)]
-            nc.vector.tensor_tensor(out=running[:], in0=bank[:], in1=running[:], op=MAX)
+            nc.vector.tensor_tensor(out=best[b, 0][:], in0=bank[:], in1=best[b, 0][:], op=MAX)
 
-        def join(b, q):
-            nc.vector.tensor_tensor(out=best[b, 0][:], in0=best[b, 0][:], in1=best[b, q][:], op=MAX)
+        def join(b, q, halves=slice(0, HALVES)):
+            nc.vector.tensor_tensor(
+                out=best[b, 0][:, halves, :], in0=best[b, 0][:, halves, :], in1=best[b, q][:, halves, :], op=MAX
+            )
 
-        def store(b):
-            nc.sync.dma_start(out=out[:, b, :].rearrange("(h p) j -> p h j", p=P), in_=best[b, 0][:])
-
-        def finish(b):
-            if PAIRS_OF[b] > 1:
-                join(b, 1)
-            store(b)
-
-        def pair_steps(b):
-            steps = []
-            for q in range(PAIRS_OF[b]):
-                steps.append((pair_difference, b, q))
-                steps.append((pair_base, b, q))
-            return steps
-
-        def run(steps, count):
-            for k in range(min(count, len(steps))):
-                step, b, q = steps[0]
-                steps.remove(steps[0])
-                step(b, q)
+        def store(b, halves=slice(0, HALVES)):
+            nc.sync.dma_start(
+                out=out[:, b, :].rearrange("(h p) j -> p h j", p=P)[:, halves, :], in_=best[b, 0][:, halves, :]
+            )
 
         for b in range(X_AHEAD):
             regroup_x(b)
             quantise_x(b)
         for b in range(4):
             project(b)
+            if b >= 2:
+                chain_start(b - 2)
             regroup_x(b + X_AHEAD)
             quantise_g(b)
             if b in neg_words:
@@ -217,39 +209,37 @@ def tile_nlgp_pa_kernel(tc, x, w_g_words, w_g_scales, out):
             quantise_x(b + X_AHEAD)
             if b in neg_words:
                 quantise_negated(b)
-        run(pair_steps(0), 2)
         regroup_x(7)
-        project(4)
-        fold(0, 2)
-        run(pair_steps(1), 2)
         quantise_x(7)
-        quantise_g(4)
+        project(4)
         project(5)
-        fold(0, 3)
-        fold(1, 2)
-        quantise_g(5)
         project(6)
-        fold(1, 3)
-        fold(0, 4)
-        fold(1, 4)
-        quantise_g(6)
+        fold(0, 1)
+        fold(1, 1)
+        quantise_g(4)
         project(7)
-        fold(0, 5)
-        fold(1, 5)
+        quantise_g(5)
+        fold(0, 2)
+        fold(1, 2)
+        quantise_g(6)
+        fold(0, 3)
         quantise_g(7)
-        ahead = []
-        for b in range(2, IMAGES):
-            ahead = ahead + pair_steps(b)
-        for s in (6, 7):
+        fold(1, 3)
+        for s in range(4, IMAGES):
             for b in (0, 1):
-                run(ahead, 1)
                 fold(b, s)
         store(0)
         store(1)
         for b0 in range(2, IMAGES, 2):
-            for s in range(2, IMAGES):
+            for b in (b0, b0 + 1):
+                pair_difference(b, 0)
+                pair_base(b, 0)
+            for s in range(2 * len(PAIRS), IMAGES):
                 for b in (b0, b0 + 1):
-                    run(ahead, 1)
                     fold(b, s)
-            store(b0)
-            store(b0 + 1)
+        for b in range(2, IMAGES):
+            pair_difference(b, 1)
+            pair_base(b, 1)
+        for b in range(2, IMAGES):
+            join(b, 1)
+            store(b)

@@ -80,8 +80,14 @@ def tile_nlgp_pa_kernel(tc, x, w_g_words, w_g_scales, out):
         g_negated = {}
 
         def regroup_x(b):
+            nc.vector.tensor_copy(**regrouping(b))
+
+        def regroup_x_on_scalar(b):
+            nc.scalar.copy(**regrouping(b))
+
+        def regrouping(b):
             x_grouped[b] = per_image.tile([P, PIXELS * PACK], BF16, name="x_grouped", align_bytes=64)
-            nc.vector.tensor_copy(
+            return dict(
                 out=x_grouped[b][:].rearrange("p (s i t) -> p s t i", i=RUN, t=PACK),
                 in_=x_raw[b][:].rearrange("p (t s i) -> p s t i", t=PACK, i=RUN),
             )
@@ -209,37 +215,44 @@ def tile_nlgp_pa_kernel(tc, x, w_g_words, w_g_scales, out):
             quantise_x(b + X_AHEAD)
             if b in neg_words:
                 quantise_negated(b)
-        regroup_x(7)
-        quantise_x(7)
+        regroup_x_on_scalar(7)
         project(4)
         project(5)
         project(6)
         fold(0, 1)
+        quantise_x(7)
         fold(1, 1)
         quantise_g(4)
         project(7)
-        quantise_g(5)
         fold(0, 2)
         fold(1, 2)
-        quantise_g(6)
+        quantise_g(5)
         fold(0, 3)
-        quantise_g(7)
+        quantise_g(6)
         fold(1, 3)
+        quantise_g(7)
         for s in range(4, IMAGES):
             for b in (0, 1):
                 fold(b, s)
         store(0)
         store(1)
+        for b in (2, 3):
+            pair_difference(b, 0)
+            pair_base(b, 0)
         for b0 in range(2, IMAGES, 2):
-            for b in (b0, b0 + 1):
-                pair_difference(b, 0)
-                pair_base(b, 0)
+            if b0 + 2 < IMAGES:
+                for b in (b0 + 2, b0 + 3):
+                    pair_difference(b, 0)
+                    pair_base(b, 0)
             for s in range(2 * len(PAIRS), IMAGES):
                 for b in (b0, b0 + 1):
                     fold(b, s)
-        for b in range(2, IMAGES):
-            pair_difference(b, 1)
-            pair_base(b, 1)
-        for b in range(2, IMAGES):
+                    if s == 5:
+                        pair_difference(b, 1)
+                        pair_base(b, 1)
+        for b in range(2, IMAGES - 1):
             join(b, 1)
             store(b)
+        for h in range(HALVES):
+            join(IMAGES - 1, 1, slice(h, h + 1))
+            store(IMAGES - 1, slice(h, h + 1))

@@ -21,6 +21,7 @@ PIXELS = 256
 HALVES = PIXELS // P
 BANK = HALVES * PIXELS
 PAIRS = ((0, 1), (2, 3))
+PAIRS_OF = (0, 0, 1, 1, 2, 2, 2, 2)
 X_AHEAD = 3
 RUN = 4
 
@@ -244,15 +245,20 @@ def tile_nlgp_pa_kernel(tc, x, w_g_words, w_g_scales, out):
                 for b in (b0 + 2, b0 + 3):
                     pair_difference(b, 0)
                     pair_base(b, 0)
-            for s in range(2 * len(PAIRS), IMAGES):
+            for s in range(2, IMAGES):
                 for b in (b0, b0 + 1):
-                    fold(b, s)
-                    if s == 5:
+                    if s >= 2 * PAIRS_OF[b]:
+                        fold(b, s)
+                    if s == 5 and PAIRS_OF[b] > 1:
                         pair_difference(b, 1)
                         pair_base(b, 1)
+            for b in (b0, b0 + 1):
+                if PAIRS_OF[b] == 1:
+                    store(b)
         for b in range(2, IMAGES - 1):
-            join(b, 1)
-            store(b)
+            if PAIRS_OF[b] > 1:
+                join(b, 1)
+                store(b)
         for h in range(HALVES):
             join(IMAGES - 1, 1, slice(h, h + 1))
             store(IMAGES - 1, slice(h, h + 1))

@@ -11,6 +11,7 @@ FP8X4 = mybir.dt.float8_e4m3fn_x4
 MAX = mybir.AluOpType.max
 MULT = mybir.AluOpType.mult
 ADD = mybir.AluOpType.add
+SUBTRACT = mybir.AluOpType.subtract
 RELU = mybir.ActivationFunctionType.Relu
 
 P = 128
@@ -21,7 +22,6 @@ PIXELS = 256
 HALVES = PIXELS // P
 BANK = HALVES * PIXELS
 PAIRS = ((0, 1), (2, 3))
-PAIRS_OF = (0, 0, 1, 1, 2, 2, 2, 2)
 X_AHEAD = 3
 RUN = 4
 
@@ -187,6 +187,10 @@ def tile_nlgp_pa_kernel(tc, x, w_g_words, w_g_scales, out):
             best[b, q] = bests.tile([P, HALVES, PIXELS], F32, name="best")
             nc.gpsimd.tensor_tensor(out=best[b, q][:], in0=excess[b, q][:], in1=base[:], op=ADD)
 
+        def pair(b, q):
+            pair_difference(b, q)
+            pair_base(b, q)
+
         def fold(b, s):
             bank = vector_banks.tile([P, HALVES, PIXELS], F32, tag="bank")
             multiply(bank, b, s)
@@ -197,14 +201,29 @@ def tile_nlgp_pa_kernel(tc, x, w_g_words, w_g_scales, out):
                 out=best[b, 0][:, halves, :], in0=best[b, 0][:, halves, :], in1=best[b, q][:, halves, :], op=MAX
             )
 
+        gap = {}
+
+        def difference_of_pairs(b):
+            gap[b] = work.tile([P, HALVES, PIXELS], F32, name="gap")
+            nc.gpsimd.tensor_tensor(out=gap[b][:], in0=best[b, 0][:], in1=best[b, 1][:], op=SUBTRACT)
+
+        def maximum_of_pairs(b):
+            lead = work.tile([P, HALVES, PIXELS], F32, name="lead")
+            nc.scalar.activation(out=lead[:], in_=gap[b][:], func=RELU)
+            best[b, 0] = bests.tile([P, HALVES, PIXELS], F32, name="best")
+            nc.gpsimd.tensor_tensor(out=best[b, 0][:], in0=lead[:], in1=best[b, 1][:], op=ADD)
+
         def store(b, halves=slice(0, HALVES)):
             nc.sync.dma_start(
                 out=out[:, b, :].rearrange("(h p) j -> p h j", p=P)[:, halves, :], in_=best[b, 0][:, halves, :]
             )
 
-        for b in range(X_AHEAD):
-            regroup_x(b)
-            quantise_x(b)
+        regroup_x(0)
+        quantise_x(0)
+        regroup_x(1)
+        regroup_x(2)
+        quantise_x(1)
+        quantise_x(2)
         for b in range(4):
             project(b)
             if b >= 2:
@@ -237,28 +256,37 @@ def tile_nlgp_pa_kernel(tc, x, w_g_words, w_g_scales, out):
                 fold(b, s)
         store(0)
         store(1)
-        for b in (2, 3):
-            pair_difference(b, 0)
-            pair_base(b, 0)
+        items = []
+        for b in (2, 3, 4, 5):
+            items.append((pair, b, 0))
+        items.append((pair, 7, 0))
+        items.append((pair, 7, 1))
+        items.append((difference_of_pairs, 7))
+        items.append((pair, 6, 0))
+        items.append((maximum_of_pairs, 7))
+        for b in (4, 5, 6):
+            items.append((pair, b, 1))
+        given = 0
+        folds = 0
         for b0 in range(2, IMAGES, 2):
-            if b0 + 2 < IMAGES:
-                for b in (b0 + 2, b0 + 3):
-                    pair_difference(b, 0)
-                    pair_base(b, 0)
-            for s in range(2, IMAGES):
+            for s in range(2 if b0 == 2 else 4, IMAGES):
                 for b in (b0, b0 + 1):
-                    if s >= 2 * PAIRS_OF[b]:
-                        fold(b, s)
-                    if s == 5 and PAIRS_OF[b] > 1:
-                        pair_difference(b, 1)
-                        pair_base(b, 1)
-            for b in (b0, b0 + 1):
-                if PAIRS_OF[b] == 1:
-                    store(b)
-        for b in range(2, IMAGES - 1):
-            if PAIRS_OF[b] > 1:
-                join(b, 1)
-                store(b)
+                    while given < min(len(items), 3 + folds * 3 // 8):
+                        item = items[given]
+                        item[0](*item[1:])
+                        given += 1
+                    fold(b, s)
+                    folds += 1
+            if b0 == 2:
+                store(2)
+                store(3)
+        for k in range(given, len(items)):
+            item = items[k]
+            item[0](*item[1:])
+        store(7)
+        for b in (4, 5):
+            join(b, 1)
+            store(b)
         for h in range(HALVES):
-            join(IMAGES - 1, 1, slice(h, h + 1))
-            store(IMAGES - 1, slice(h, h + 1))
+            join(6, 1, slice(h, h + 1))
+            store(6, slice(h, h + 1))

@@ -56,22 +56,28 @@ def tile_nlgp_pa_kernel(tc, x, w_g_words, w_g_scales, out):
         nc.vector.memset(w_scales[:].bitcast(I32), 0)
         nc.vector.memset(warm[:], 0.0)
         nc.scalar.activation(out=warm[:], in_=warm[:], func=RELU)
-        x_by_word = x.rearrange("b (p t) h w -> p b (t h w)", t=PACK)
+        x_by_word = x.rearrange("b (p t) h w -> p b t (h w)", t=PACK)
         x_raw = []
         for b in range(IMAGES):
             raw = per_image.tile([P, PACK * PIXELS], BF16, name="x_raw")
-            nc.sync.dma_start(out=raw[:], in_=x_by_word[:, b, :])
             x_raw.append(raw)
-            if b == 0:
-                for quadrant in range(4):
-                    nc.sync.dma_start(
-                        out=w_scales[32 * quadrant : 32 * quadrant + 4, :].bitcast(I32),
-                        in_=w_g_scales[0, 4 * quadrant : 4 * quadrant + 4, :].bitcast(I32),
-                    )
-                nc.sync.dma_start(
-                    out=w_words[:].bitcast(I32),
-                    in_=w_g_words[0].rearrange("p d t -> p (d t)").bitcast(I32),
-                )
+        nc.sync.dma_start(out=x_raw[0][:].rearrange("p (t i) -> p t i", t=PACK), in_=x_by_word[:, 0, :, :])
+        nc.sync.dma_start(out=x_raw[1][:].rearrange("p (t i) -> p t i", t=PACK), in_=x_by_word[:, 1, :, :])
+        for quadrant in range(4):
+            nc.sync.dma_start(
+                out=w_scales[32 * quadrant : 32 * quadrant + 4, :].bitcast(I32),
+                in_=w_g_scales[0, 4 * quadrant : 4 * quadrant + 4, :].bitcast(I32),
+            )
+        nc.sync.dma_start(
+            out=w_words[:].bitcast(I32),
+            in_=w_g_words[0].rearrange("p d t -> p (d t)").bitcast(I32),
+        )
+        nc.sync.dma_start(out=x_raw[2][:].rearrange("p (t i) -> p t i", t=PACK), in_=x_by_word[:, 2, :, :])
+        nc.sync.dma_start(out=x_raw[3][:].rearrange("p (t i) -> p t i", t=PACK), in_=x_by_word[:, 3, :, :])
+        nc.sync.dma_start(out=x_raw[4][:].rearrange("p (t i) -> p t i", t=PACK), in_=x_by_word[:, 4, :, :])
+        nc.sync.dma_start(out=x_raw[5][:].rearrange("p (t i) -> p t i", t=PACK), in_=x_by_word[:, 5, :, :])
+        nc.sync.dma_start(out=x_raw[6][:].rearrange("p (t i) -> p t i", t=PACK), in_=x_by_word[:, 6, :, :])
+        nc.sync.dma_start(out=x_raw[7][:].rearrange("p (t i) -> p t i", t=PACK), in_=x_by_word[:, 7, :, :])
 
         def image_columns(b):
             return slice(b * PIXELS, (b + 1) * PIXELS)
@@ -91,6 +97,23 @@ def tile_nlgp_pa_kernel(tc, x, w_g_words, w_g_scales, out):
             return dict(
                 out=x_grouped[b][:].rearrange("p (s i t) -> p s t i", i=RUN, t=PACK),
                 in_=x_raw[b][:].rearrange("p (t s i) -> p s t i", t=PACK, i=RUN),
+            )
+
+        def regroup_half(h):
+            if h == 0:
+                x_grouped[0] = per_image.tile([P, PIXELS * PACK], BF16, name="x_grouped", align_bytes=64)
+            n = PIXELS // 2
+            nc.vector.tensor_copy(
+                out=x_grouped[0][:, h * n * PACK : (h + 1) * n * PACK].rearrange("p (s i t) -> p s t i", i=RUN, t=PACK),
+                in_=x_raw[0][:].rearrange("p (t g s i) -> p g s t i", t=PACK, g=2, i=RUN)[:, h],
+            )
+
+        def quantise_half(h):
+            n = PIXELS // 2
+            nc.vector.quantize_mx(
+                out=x_words[:, h * n : (h + 1) * n].bitcast(FP8X4),
+                scales=x_scales[:, h * n : (h + 1) * n],
+                in_=x_grouped[0][:, h * n * PACK : (h + 1) * n * PACK],
             )
 
         def quantise_x(b):
@@ -218,8 +241,10 @@ def tile_nlgp_pa_kernel(tc, x, w_g_words, w_g_scales, out):
                 out=out[:, b, :].rearrange("(h p) j -> p h j", p=P)[:, halves, :], in_=best[b, 0][:, halves, :]
             )
 
-        regroup_x(0)
-        quantise_x(0)
+        for h in range(2):
+            regroup_half(h)
+        for h in range(2):
+            quantise_half(h)
         regroup_x(1)
         regroup_x(2)
         quantise_x(1)

@@ -249,11 +249,13 @@ def tile_nlgp_pa_kernel(tc, x, w_g_words, w_g_scales, out):
         regroup_x(2)
         quantise_x(1)
         quantise_x(2)
+        regroup_x(3)
         for b in range(4):
             project(b)
             if b >= 2:
                 chain_start(b - 2)
-            regroup_x(b + X_AHEAD)
+            if b < 3:
+                regroup_x(b + 4)
             quantise_g(b)
             if b in neg_words:
                 negate_g(b)
@@ -282,33 +284,35 @@ def tile_nlgp_pa_kernel(tc, x, w_g_words, w_g_scales, out):
         store(0)
         store(1)
         items = []
-        for b in (2, 3, 4, 5):
+        for b in (2, 3, 7):
             items.append((pair, b, 0))
-        items.append((pair, 7, 0))
         items.append((pair, 7, 1))
         items.append((difference_of_pairs, 7))
-        items.append((pair, 6, 0))
+        items.append((pair, 4, 0))
         items.append((maximum_of_pairs, 7))
+        for b in (5, 6):
+            items.append((pair, b, 0))
         for b in (4, 5, 6):
             items.append((pair, b, 1))
         given = 0
         folds = 0
-        for b0 in range(2, IMAGES, 2):
-            for s in range(2 if b0 == 2 else 4, IMAGES):
-                for b in (b0, b0 + 1):
+        for rows in ((2, 3), (4, 7), (5, 6)):
+            for s in range(2 if rows[0] == 2 else 4, IMAGES):
+                for b in rows:
                     while given < min(len(items), 3 + folds * 3 // 8):
                         item = items[given]
                         item[0](*item[1:])
                         given += 1
                     fold(b, s)
                     folds += 1
-            if b0 == 2:
+            if rows[0] == 2:
                 store(2)
                 store(3)
+            if rows[1] == 7:
+                store(7)
         for k in range(given, len(items)):
             item = items[k]
             item[0](*item[1:])
-        store(7)
         for b in (4, 5):
             join(b, 1)
             store(b)

from contextlib import ExitStack

import concourse.mybir as mybir

BF16 = mybir.dt.bfloat16
F32 = mybir.dt.float32
I32 = mybir.dt.int32
U32 = mybir.dt.uint32
U8 = mybir.dt.uint8
FP8X4 = mybir.dt.float8_e4m3fn_x4
MAX = mybir.AluOpType.max
MULT = mybir.AluOpType.mult
ADD = mybir.AluOpType.add
SUBTRACT = mybir.AluOpType.subtract
RELU = mybir.ActivationFunctionType.Relu

P = 128
PACK = 4
IMAGES = 8
CHANNELS = P * PACK
PIXELS = 256
HALVES = PIXELS // P
BANK = HALVES * PIXELS
PAIRS = ((0, 1), (2, 3))
X_AHEAD = 3
RUN = 4

FLOPS = 2 * IMAGES * PIXELS * CHANNELS * CHANNELS + 2 * (IMAGES * PIXELS) ** 2 * CHANNELS


def tile_nlgp_pa_kernel(tc, x, w_g_words, w_g_scales, out):
    nc = tc.nc
    with ExitStack() as ctx:
        pinned = {mybir.EngineType.DVE, mybir.EngineType.Activation, mybir.EngineType.Pool}
        ctx.enter_context(tc.manual_schedule(engines=pinned))
        keep = ctx.enter_context(tc.tile_pool(name="keep", bufs=1))
        per_image = ctx.enter_context(tc.tile_pool(name="per_image", bufs=IMAGES))
        work = ctx.enter_context(tc.tile_pool(name="work", bufs=4))
        bests = ctx.enter_context(tc.tile_pool(name="bests", bufs=16))
        scalar_banks = ctx.enter_context(tc.psum_pool(name="scalar_banks", bufs=4))
        vector_banks = ctx.enter_context(tc.psum_pool(name="vector_banks", bufs=4))

        w_words = keep.tile([P, CHANNELS], U32, align_bytes=64)
        w_scales = keep.tile([P, CHANNELS], U8, align_bytes=64)
        x_words = keep.tile([P, IMAGES * PIXELS], U32, align_bytes=64)
        x_scales = keep.tile([P, IMAGES * PIXELS], U8, align_bytes=64)
        g_words = keep.tile([P, IMAGES * PIXELS], U32, align_bytes=64)
        g_scales = keep.tile([P, IMAGES * PIXELS], U8, align_bytes=64)
        neg_words = {}
        neg_scales = {}
        for pair in PAIRS:
            neg_words[pair[1]] = keep.tile([P, PIXELS], U32, name="neg_words%d" % pair[1], align_bytes=64)
            neg_scales[pair[1]] = keep.tile([P, PIXELS], U8, name="neg_scales%d" % pair[1], align_bytes=64)
        warm = keep.tile([P, 8], F32)

        nc.vector.memset(w_scales[:].bitcast(I32), 0)
        nc.vector.memset(warm[:], 0.0)
        nc.scalar.activation(out=warm[:], in_=warm[:], func=RELU)
        x_by_word = x.rearrange("b (p t) h w -> p b t (h w)", t=PACK)
        x_raw = []
        for b in range(IMAGES):
            raw = per_image.tile([P, PACK * PIXELS], BF16, name="x_raw")
            x_raw.append(raw)
        nc.sync.dma_start(out=x_raw[0][:].rearrange("p (t i) -> p t i", t=PACK), in_=x_by_word[:, 0, :, :])
        nc.sync.dma_start(out=x_raw[1][:].rearrange("p (t i) -> p t i", t=PACK), in_=x_by_word[:, 1, :, :])
        for quadrant in range(4):
            nc.sync.dma_start(
                out=w_scales[32 * quadrant : 32 * quadrant + 4, :].bitcast(I32),
                in_=w_g_scales[0, 4 * quadrant : 4 * quadrant + 4, :].bitcast(I32),
            )
        nc.sync.dma_start(
            out=w_words[:].bitcast(I32),
            in_=w_g_words[0].rearrange("p d t -> p (d t)").bitcast(I32),
        )
        nc.sync.dma_start(out=x_raw[2][:].rearrange("p (t i) -> p t i", t=PACK), in_=x_by_word[:, 2, :, :])
        nc.sync.dma_start(out=x_raw[3][:].rearrange("p (t i) -> p t i", t=PACK), in_=x_by_word[:, 3, :, :])
        nc.sync.dma_start(out=x_raw[4][:].rearrange("p (t i) -> p t i", t=PACK), in_=x_by_word[:, 4, :, :])
        nc.sync.dma_start(out=x_raw[5][:].rearrange("p (t i) -> p t i", t=PACK), in_=x_by_word[:, 5, :, :])
        nc.sync.dma_start(out=x_raw[6][:].rearrange("p (t i) -> p t i", t=PACK), in_=x_by_word[:, 6, :, :])
        nc.sync.dma_start(out=x_raw[7][:].rearrange("p (t i) -> p t i", t=PACK), in_=x_by_word[:, 7, :, :])

        def image_columns(b):
            return slice(b * PIXELS, (b + 1) * PIXELS)

        x_grouped = {}
        g_grouped = {}
        g_negated = {}

        def regroup_x(b):
            nc.vector.tensor_copy(**regrouping(b))

        def regroup_x_on_scalar(b):
            nc.scalar.copy(**regrouping(b))

        def regrouping(b):
            x_grouped[b] = per_image.tile([P, PIXELS * PACK], BF16, name="x_grouped", align_bytes=64)
            return dict(
                out=x_grouped[b][:].rearrange("p (s i t) -> p s t i", i=RUN, t=PACK),
                in_=x_raw[b][:].rearrange("p (t s i) -> p s t i", t=PACK, i=RUN),
            )

        def regroup_half(h):
            if h == 0:
                x_grouped[0] = per_image.tile([P, PIXELS * PACK], BF16, name="x_grouped", align_bytes=64)
            n = PIXELS // 2
            nc.vector.tensor_copy(
                out=x_grouped[0][:, h * n * PACK : (h + 1) * n * PACK].rearrange("p (s i t) -> p s t i", i=RUN, t=PACK),
                in_=x_raw[0][:].rearrange("p (t g s i) -> p g s t i", t=PACK, g=2, i=RUN)[:, h],
            )

        def quantise_half(h):
            n = PIXELS // 2
            nc.vector.quantize_mx(
                out=x_words[:, h * n : (h + 1) * n].bitcast(FP8X4),
                scales=x_scales[:, h * n : (h + 1) * n],
                in_=x_grouped[0][:, h * n * PACK : (h + 1) * n * PACK],
            )

        def quantise_x(b):
            nc.vector.quantize_mx(
                out=x_words[:, image_columns(b)].bitcast(FP8X4),
                scales=x_scales[:, image_columns(b)],
                in_=x_grouped[b][:],
            )

        def project(b):
            g_grouped[b] = per_image.tile([P, PIXELS, PACK], BF16, name="g_grouped", align_bytes=64)
            for h in range(HALVES):
                bank = scalar_banks.tile([P, PACK, P], F32, tag="bank")
                pixels = slice(b * PIXELS + h * P, b * PIXELS + (h + 1) * P)
                for t in range(PACK):
                    d_tile = slice(t * P, (t + 1) * P)
                    nc.tensor.matmul_mx(
                        out=bank[:, t, :],
                        lhsT=w_words[:, d_tile].bitcast(FP8X4),
                        lhsT_scale=w_scales[:, d_tile],
                        rhs=x_words[:, pixels].bitcast(FP8X4),
                        rhs_scale=x_scales[:, pixels],
                        start=True,
                        stop=True,
                    )
                nc.scalar.copy(
                    out=g_grouped[b][:, h * P : (h + 1) * P, :],
                    in_=bank[:].rearrange("p t i -> p i t"),
                )

        def quantise_g(b):
            nc.vector.quantize_mx(
                out=g_words[:, image_columns(b)].bitcast(FP8X4),
                scales=g_scales[:, image_columns(b)],
                in_=g_grouped[b][:].rearrange("p i t -> p (i t)"),
            )

        def negate_g(b):
            g_negated[b] = keep.tile([P, PIXELS * PACK], BF16, name="g_negated%d" % b, align_bytes=64)
            nc.vector.tensor_scalar(
                out=g_negated[b][:], in0=g_grouped[b][:].rearrange("p i t -> p (i t)"), scalar1=-1.0, scalar2=None, op0=MULT
            )

        def quantise_negated(b):
            nc.vector.quantize_mx(
                out=neg_words[b][:].bitcast(FP8X4),
                scales=neg_scales[b][:],
                in_=g_negated[b][:],
            )

        def multiply(bank, b, partner, minus=None):
            for h in range(HALVES):
                rows = slice(b * PIXELS + h * P, b * PIXELS + (h + 1) * P)
                nc.tensor.matmul_mx(
                    out=bank[:, h, :],
                    lhsT=g_words[:, rows].bitcast(FP8X4),
                    lhsT_scale=g_scales[:, rows],
                    rhs=g_words[:, image_columns(partner)].bitcast(FP8X4),
                    rhs_scale=g_scales[:, image_columns(partner)],
                    start=True,
                    stop=minus is None,
                )
                if minus is not None:
                    nc.tensor.matmul_mx(
                        out=bank[:, h, :],
                        lhsT=g_words[:, rows].bitcast(FP8X4),
                        lhsT_scale=g_scales[:, rows],
                        rhs=neg_words[minus][:].bitcast(FP8X4),
                        rhs_scale=neg_scales[minus][:],
                        start=False,
                        stop=True,
                    )

        excess = {}
        best = {}

        def chain_start(b):
            bank = scalar_banks.tile([P, HALVES, PIXELS], F32, tag="bank")
            multiply(bank, b, 0)
            best[b, 0] = bests.tile([P, HALVES, PIXELS], F32, name="best")
            nc.scalar.copy(out=best[b, 0][:], in_=bank[:])

        def pair_difference(b, q):
            bank = scalar_banks.tile([P, HALVES, PIXELS], F32, tag="bank")
            multiply(bank, b, PAIRS[q][0], minus=PAIRS[q][1])
            excess[b, q] = work.tile([P, HALVES, PIXELS], F32, name="excess")
            nc.scalar.activation(out=excess[b, q][:], in_=bank[:], func=RELU)

        def pair_base(b, q):
            bank = scalar_banks.tile([P, HALVES, PIXELS], F32, tag="bank")
            multiply(bank, b, PAIRS[q][1])
            base = work.tile([P, HALVES, PIXELS], F32, name="base")
            nc.scalar.copy(out=base[:], in_=bank[:])
            best[b, q] = bests.tile([P, HALVES, PIXELS], F32, name="best")
            nc.gpsimd.tensor_tensor(out=best[b, q][:], in0=excess[b, q][:], in1=base[:], op=ADD)

        def pair(b, q):
            pair_difference(b, q)
            pair_base(b, q)

        def fold(b, s):
            bank = vector_banks.tile([P, HALVES, PIXELS], F32, tag="bank")
            multiply(bank, b, s)
            nc.vector.tensor_tensor(out=best[b, 0][:], in0=bank[:], in1=best[b, 0][:], op=MAX)

        def join(b, q, halves=slice(0, HALVES)):
            nc.vector.tensor_tensor(
                out=best[b, 0][:, halves, :], in0=best[b, 0][:, halves, :], in1=best[b, q][:, halves, :], op=MAX
            )

        gap = {}

        def difference_of_pairs(b):
            gap[b] = work.tile([P, HALVES, PIXELS], F32, name="gap")
            nc.gpsimd.tensor_tensor(out=gap[b][:], in0=best[b, 0][:], in1=best[b, 1][:], op=SUBTRACT)

        def maximum_of_pairs(b):
            lead = work.tile([P, HALVES, PIXELS], F32, name="lead")
            nc.scalar.activation(out=lead[:], in_=gap[b][:], func=RELU)
            best[b, 0] = bests.tile([P, HALVES, PIXELS], F32, name="best")
            nc.gpsimd.tensor_tensor(out=best[b, 0][:], in0=lead[:], in1=best[b, 1][:], op=ADD)

        def store(b, halves=slice(0, HALVES)):
            nc.sync.dma_start(
                out=out[:, b, :].rearrange("(h p) j -> p h j", p=P)[:, halves, :], in_=best[b, 0][:, halves, :]
            )

        for h in range(2):
            regroup_half(h)
        for h in range(2):
            quantise_half(h)
        regroup_x(1)
        regroup_x(2)
        quantise_x(1)
        quantise_x(2)
        regroup_x(3)
        for b in range(4):
            project(b)
            if b >= 2:
                chain_start(b - 2)
            if b < 3:
                regroup_x(b + 4)
            quantise_g(b)
            if b in neg_words:
                negate_g(b)
            quantise_x(b + X_AHEAD)
            if b in neg_words:
                quantise_negated(b)
        regroup_x_on_scalar(7)
        project(4)
        project(5)
        project(6)
        fold(0, 1)
        quantise_x(7)
        fold(1, 1)
        quantise_g(4)
        project(7)
        fold(0, 2)
        fold(1, 2)
        quantise_g(5)
        fold(0, 3)
        quantise_g(6)
        fold(1, 3)
        quantise_g(7)
        for s in range(4, IMAGES):
            for b in (0, 1):
                fold(b, s)
        store(0)
        store(1)
        items = []
        for b in (2, 3, 7):
            items.append((pair, b, 0))
        items.append((pair, 7, 1))
        items.append((difference_of_pairs, 7))
        items.append((pair, 4, 0))
        items.append((maximum_of_pairs, 7))
        for b in (5, 6):
            items.append((pair, b, 0))
        for b in (4, 5, 6):
            items.append((pair, b, 1))
        given = 0
        folds = 0
        for rows in ((2, 3), (4, 7), (5, 6)):
            for s in range(2 if rows[0] == 2 else 4, IMAGES):
                for b in rows:
                    while given < min(len(items), 3 + folds * 3 // 8):
                        item = items[given]
                        item[0](*item[1:])
                        given += 1
                    fold(b, s)
                    folds += 1
            if rows[0] == 2:
                store(2)
                store(3)
            if rows[1] == 7:
                store(7)
        for k in range(given, len(items)):
            item = items[k]
            item[0](*item[1:])
        for b in (4, 5):
            join(b, 1)
            store(b)
        for h in range(HALVES):
            join(6, 1, slice(h, h + 1))
            store(6, slice(h, h + 1))
